import numpy as np
import ml_dtypes


def mxq(x, axis, fmt="e4m3"):
    dtype, down = {"e4m3": (ml_dtypes.float8_e4m3fn, 7), "e5m2": (ml_dtypes.float8_e5m2, 14)}[fmt]
    v = np.moveaxis(np.asarray(x, np.float32).astype(ml_dtypes.bfloat16).astype(np.float64), axis, -1)
    blocks = v.reshape(v.shape[:-1] + (-1, 32))
    amax = np.abs(blocks).max(-1, keepdims=True)
    byte = np.maximum(np.where(amax > 0, np.frexp(amax)[1] - 1 + 127, 0) - down, 1)
    scale = np.exp2(byte - 127.0)
    codes = (blocks / scale).astype(np.float32).astype(dtype).astype(np.float64)
    return np.moveaxis((codes * scale).reshape(v.shape), -1, axis)


WIDE = False


def mx_kscale(k):
    if not WIDE:
        return np.ones(k)
    levels = np.array([20, -20, 10, -10, 0])
    a = np.random.permutation(np.resize(levels, k // 512 * 4)).reshape(k // 512, 4)
    idx = np.arange(k)
    return np.exp2(a[idx // 512, idx % 128 // 32])


BF16 = ml_dtypes.bfloat16


def bf(x):
    return np.asarray(x, np.float32).astype(BF16)


def f64(x):
    return np.asarray(x).astype(np.float64)


B, S, D_IN, D_OUT = 4, 4096, 512, 512
T = B * S


def relative_shift(x):
    b, s, d = x.shape
    padded = np.concatenate([np.zeros((b, 1, d)), x], axis=1).reshape(s + 1, b, d)
    return padded[1:].reshape(b, s, d)


def setup_inputs():
    sv = mx_kscale(T)
    idx = (S + 1) * np.arange(B)[:, None] + np.arange(S)[None, :] + 1 - B
    fac = np.where(idx >= 0, sv[np.maximum(idx, 0)], 1.0)[:, :, None]
    pos_embed = np.random.standard_normal((B, S, D_IN)) * fac
    W_r = np.random.standard_normal((D_OUT, D_IN)) * 1.2 / np.sqrt(D_IN)
    b_r = np.random.standard_normal(D_OUT) * 0.3
    g = np.random.standard_normal((B, S, D_OUT)) * np.exp2(np.random.randint(-12, 1, (B, S, 1))) / sv.reshape(B, S, 1)
    return {"pos_embed": bf(pos_embed), "W_r": bf(W_r), "b_r": bf(b_r), "grad_out": bf(g)}


def reference(pos_embed, W_r, b_r, grad_out):
    shifted = relative_shift(f64(pos_embed)).reshape(T, D_IN)
    g = f64(grad_out).reshape(T, D_OUT)
    return mxq(g, 0, "e5m2").T @ mxq(shifted, 0, "e4m3")

@@ -1,0 +1,195 @@
+from contextlib import ExitStack
+
+import concourse.mybir as mybir
+from concourse.masks import make_identity
+
+BF16 = mybir.dt.bfloat16
+F32 = mybir.dt.float32
+U32 = mybir.dt.uint32
+U8 = mybir.dt.uint8
+E4M3_X4 = mybir.dt.float8_e4m3fn_x4
+E5M2_X4 = mybir.dt.float8_e5m2_x4
+
+B, S, D_IN, D_OUT = 4, 4096, 512, 512
+T = B * S
+P = 128
+PACK = 4
+K_PASS = P * PACK
+PASSES = T // K_PASS
+PASSES_PER_BATCH = S // K_PASS
+M_TILES = D_OUT // P
+RUN = 4
+
+X_LOAD_LEAD = 3
+PATCH_LAG = 2
+X_REGROUP_LEAD = X_LOAD_LEAD - PATCH_LAG
+
+X_RAW_BUFS = 6
+G_RAW_BUFS = 4
+WORK_BUFS = 3
+
+FLOPS = 2 * T * D_OUT * D_IN
+BYTES = 2 * T * D_OUT + 2 * (T - (B - 1)) * D_IN + 4 * D_OUT * D_IN
+
+assert B - 1 < PACK
+
+
+def lag_of(c):
+    return B - 1 - c // PASSES_PER_BATCH
+
+
+def is_seam(c):
+    return (c + 1) % PASSES_PER_BATCH == 0 and lag_of(c) > 0
+
+
+def regrouped_views(grouped, raw):
+    return (
+        grouped[:].rearrange("p (c i) j -> p c j i", i=RUN),
+        raw[:].rearrange("p j (c i) -> p c j i", i=RUN),
+    )
+
+
+def tile_relativemultiheadattention_pa_k_kernel(tc, pos_embed, W_r, b_r, grad_out, out):
+    nc = tc.nc
+    g_rows = grad_out.flatten_outer_dims()
+    e_rows = pos_embed.flatten_outer_dims()
+
+    with ExitStack() as stack:
+        const = stack.enter_context(tc.tile_pool(name="const", bufs=1))
+        x_raw_pool = stack.enter_context(tc.tile_pool(name="x_raw_pool", bufs=X_RAW_BUFS))
+        g_raw_pool = stack.enter_context(tc.tile_pool(name="g_raw_pool", bufs=G_RAW_BUFS))
+        work = stack.enter_context(tc.tile_pool(name="work", bufs=WORK_BUFS))
+        results = stack.enter_context(tc.tile_pool(name="results", bufs=M_TILES))
+        psum = stack.enter_context(tc.psum_pool(name="psum", bufs=1))
+        stack.enter_context(tc.manual_schedule())
+
+        identity = const.tile([P, P], F32)
+        make_identity(nc, identity[:])
+        keep = const.tile([P, 1], F32)
+        nc.vector.tensor_scalar(
+            out=keep[:],
+            in0=identity[:, P - 1 : P],
+            scalar1=-1.0,
+            scalar2=1.0,
+            op0=mybir.AluOpType.mult,
+            op1=mybir.AluOpType.add,
+        )
+
+        acc = []
+        for m in range(M_TILES):
+            acc.append(psum.tile([P, D_IN], F32, name="acc%d" % m))
+
+        x_raw_of, x_grouped_of, x_mx_of = {}, {}, {}
+        g_raw_of, g_grouped_of, g_mx_of = {}, {}, {}
+
+        def in_range(c):
+            return 0 <= c < PASSES
+
+        def load_x(c):
+            if not in_range(c):
+                return
+            x_raw = x_raw_pool.tile([P, PACK, D_IN], BF16)
+            first = c * K_PASS + lag_of(c)
+            nc.sync.dma_start(
+                out=x_raw[:], in_=e_rows[first : first + K_PASS, :].rearrange("(p j) w -> p j w", j=PACK)
+            )
+            x_raw_of[c] = x_raw
+
+        def patch_x(c):
+            if not in_range(c) or not is_seam(c) or lag_of(c) == 1:
+                return
+            behind = lag_of(c) - 1
+            next_batch = (c + 1) * K_PASS
+            nc.sync.dma_start(
+                out=x_raw_of[c][P - 1 : P, PACK - behind : PACK, :],
+                in_=e_rows[next_batch : next_batch + behind, :].rearrange("(o j) w -> o j w", o=1),
+            )
+
+        def regroup_x(c):
+            if not in_range(c):
+                return
+            x_raw = x_raw_of[c]
+            if is_seam(c):
+                zero_j = PACK - lag_of(c)
+                nc.vector.tensor_scalar_mul(out=x_raw[:, zero_j, :], in0=x_raw[:, zero_j, :], scalar1=keep[:, 0:1])
+            x_grouped = work.tile([P, D_IN, PACK], BF16, align_bytes=64)
+            to_view, from_view = regrouped_views(x_grouped, x_raw)
+            nc.vector.tensor_copy(out=to_view, in_=from_view)
+            x_grouped_of[c] = x_grouped
+
+        def quantise_x(c):
+            if not in_range(c):
+                return
+            x_words = work.tile([P, D_IN], U32, align_bytes=64)
+            x_scales = work.tile([P, D_IN], U8, align_bytes=64)
+            nc.vector.quantize_mx(
+                out=x_words[:].bitcast(E4M3_X4),
+                scales=x_scales[:],
+                in_=x_grouped_of[c][:].rearrange("p w j -> p (w j)"),
+            )
+            x_mx_of[c] = (x_words, x_scales)
+
+        def load_g(c):
+            if not in_range(c):
+                return
+            g_raw = g_raw_pool.tile([P, PACK, D_OUT], BF16)
+            first = c * K_PASS
+            nc.sync.dma_start(
+                out=g_raw[:], in_=g_rows[first : first + K_PASS, :].rearrange("(p j) w -> p j w", j=PACK)
+            )
+            g_raw_of[c] = g_raw
+
+        def regroup_g(c):
+            if not in_range(c):
+                return
+            g_grouped = work.tile([P, D_OUT, PACK], BF16, align_bytes=64)
+            to_view, from_view = regrouped_views(g_grouped, g_raw_of[c])
+            nc.scalar.copy(out=to_view, in_=from_view)
+            g_grouped_of[c] = g_grouped
+
+        def quantise_g(c):
+            if not in_range(c):
+                return
+            g_words = work.tile([P, D_OUT], U32, align_bytes=64)
+            g_scales = work.tile([P, D_OUT], U8, align_bytes=64)
+            nc.vector.quantize_mx(
+                out=g_words[:].bitcast(E5M2_X4),
+                scales=g_scales[:],
+                in_=g_grouped_of[c][:].rearrange("p w j -> p (w j)"),
+            )
+            g_mx_of[c] = (g_words, g_scales)
+
+        def multiply(c):
+            if not in_range(c):
+                return
+            g_words, g_scales = g_mx_of[c]
+            x_words, x_scales = x_mx_of[c]
+            for m in range(M_TILES):
+                m_cols = slice(m * P, (m + 1) * P)
+                nc.tensor.matmul_mx(
+                    out=acc[m][:],
+                    lhsT=g_words[:, m_cols].bitcast(E5M2_X4),
+                    lhsT_scale=g_scales[:, m_cols],
+                    rhs=x_words[:].bitcast(E4M3_X4),
+                    rhs_scale=x_scales[:],
+                    start=(c == 0),
+                    stop=(c == PASSES - 1),
+                )
+
+        for c in range(-X_LOAD_LEAD, PASSES):
+            load_x(c + X_LOAD_LEAD)
+            patch_x(c + X_REGROUP_LEAD)
+            load_g(c)
+            regroup_g(c)
+            regroup_x(c + X_REGROUP_LEAD)
+            quantise_x(c)
+            quantise_g(c)
+            multiply(c)
+
+        for m in range(M_TILES):
+            result = results.tile([P, D_IN], F32)
+            if m % 2 == 0:
+                nc.vector.tensor_copy(out=result[:], in_=acc[m][:])
+            else:
+                nc.scalar.copy(out=result[:], in_=acc[m][:])
+            nc.sync.dma_start(out=out[m * P : (m + 1) * P, :], in_=result[:])

@@ -20,12 +20,10 @@ PASSES_PER_BATCH = S // K_PASS
 M_TILES = D_OUT // P
 RUN = 4
 
-X_LOAD_LEAD = 3
+SEAM_LEAD = 4
 PATCH_LAG = 2
-X_REGROUP_LEAD = X_LOAD_LEAD - PATCH_LAG
 
-X_RAW_BUFS = 6
-G_RAW_BUFS = 4
+RAW_BUFS = 5
 WORK_BUFS = 3
 
 FLOPS = 2 * T * D_OUT * D_IN
@@ -56,8 +54,8 @@ def tile_relativemultiheadattention_pa_k_kernel(tc, pos_embed, W_r, b_r, grad_ou
 
     with ExitStack() as stack:
         const = stack.enter_context(tc.tile_pool(name="const", bufs=1))
-        x_raw_pool = stack.enter_context(tc.tile_pool(name="x_raw_pool", bufs=X_RAW_BUFS))
-        g_raw_pool = stack.enter_context(tc.tile_pool(name="g_raw_pool", bufs=G_RAW_BUFS))
+        raw_pool = stack.enter_context(tc.tile_pool(name="raw_pool", bufs=RAW_BUFS))
+        seam_pool = stack.enter_context(tc.tile_pool(name="seam_pool", bufs=1))
         work = stack.enter_context(tc.tile_pool(name="work", bufs=WORK_BUFS))
         results = stack.enter_context(tc.tile_pool(name="results", bufs=M_TILES))
         psum = stack.enter_context(tc.psum_pool(name="psum", bufs=1))
@@ -88,7 +86,8 @@ def tile_relativemultiheadattention_pa_k_kernel(tc, pos_embed, W_r, b_r, grad_ou
         def load_x(c):
             if not in_range(c):
                 return
-            x_raw = x_raw_pool.tile([P, PACK, D_IN], BF16)
+            pool = seam_pool if is_seam(c) else raw_pool
+            x_raw = pool.tile([P, PACK, D_IN], BF16)
             first = c * K_PASS + lag_of(c)
             nc.sync.dma_start(
                 out=x_raw[:], in_=e_rows[first : first + K_PASS, :].rearrange("(p j) w -> p j w", j=PACK)
@@ -132,7 +131,7 @@ def tile_relativemultiheadattention_pa_k_kernel(tc, pos_embed, W_r, b_r, grad_ou
         def load_g(c):
             if not in_range(c):
                 return
-            g_raw = g_raw_pool.tile([P, PACK, D_OUT], BF16)
+            g_raw = raw_pool.tile([P, PACK, D_OUT], BF16)
             first = c * K_PASS
             nc.sync.dma_start(
                 out=g_raw[:], in_=g_rows[first : first + K_PASS, :].rearrange("(p j) w -> p j w", j=PACK)
@@ -176,12 +175,15 @@ def tile_relativemultiheadattention_pa_k_kernel(tc, pos_embed, W_r, b_r, grad_ou
                     stop=(c == PASSES - 1),
                 )
 
-        for c in range(-X_LOAD_LEAD, PASSES):
-            load_x(c + X_LOAD_LEAD)
-            patch_x(c + X_REGROUP_LEAD)
-            load_g(c)
+        for c in range(-1, PASSES):
+            if not is_seam(c + 1):
+                load_x(c + 1)
+            load_g(c + 1)
+            if is_seam(c + 1 + SEAM_LEAD):
+                load_x(c + 1 + SEAM_LEAD)
+            patch_x(c + 1 + SEAM_LEAD - PATCH_LAG)
             regroup_g(c)
-            regroup_x(c + X_REGROUP_LEAD)
+            regroup_x(c + 1)
             quantise_x(c)
             quantise_g(c)
             multiply(c)

@@ -20,11 +20,19 @@ PASSES_PER_BATCH = S // K_PASS
 M_TILES = D_OUT // P
 RUN = 4
 
+PE_COLS = 192
+V_COLS = 432
+STAGE_COLS = 256
+FORM = 2
+
+LOAD_LEAD = 3
+STAGE_LEAD = 2
 SEAM_LEAD = 4
 PATCH_LAG = 2
 
-RAW_BUFS = 5
-WORK_BUFS = 3
+RAW_BUFS = 6
+WORK_BUFS = 4
+STAGE_BUFS = 4
 
 FLOPS = 2 * T * D_OUT * D_IN
 BYTES = 2 * T * D_OUT + 2 * (T - (B - 1)) * D_IN + 4 * D_OUT * D_IN
@@ -40,10 +48,10 @@ def is_seam(c):
     return (c + 1) % PASSES_PER_BATCH == 0 and lag_of(c) > 0
 
 
-def regrouped_views(grouped, raw):
+def regrouped_views(grouped, raw, lo, hi):
     return (
-        grouped[:].rearrange("p (c i) j -> p c j i", i=RUN),
-        raw[:].rearrange("p j (c i) -> p c j i", i=RUN),
+        grouped[:, lo:hi, :].rearrange("p (c i) j -> p c j i", i=RUN),
+        raw[:, :, lo:hi].rearrange("p j (c i) -> p c j i", i=RUN),
     )
 
 
@@ -59,9 +67,10 @@ def tile_relativemultiheadattention_pa_k_kernel(tc, pos_embed, W_r, b_r, grad_ou
         work = stack.enter_context(tc.tile_pool(name="work", bufs=WORK_BUFS))
         results = stack.enter_context(tc.tile_pool(name="results", bufs=M_TILES))
         psum = stack.enter_context(tc.psum_pool(name="psum", bufs=1))
+        stage_pool = stack.enter_context(tc.psum_pool(name="stage_pool", bufs=STAGE_BUFS))
         stack.enter_context(tc.manual_schedule())
 
-        identity = const.tile([P, P], F32)
+        identity = const.tile([P, P], BF16)
         make_identity(nc, identity[:])
         keep = const.tile([P, 1], F32)
         nc.vector.tensor_scalar(
@@ -78,7 +87,7 @@ def tile_relativemultiheadattention_pa_k_kernel(tc, pos_embed, W_r, b_r, grad_ou
             acc.append(psum.tile([P, D_IN], F32, name="acc%d" % m))
 
         x_raw_of, x_grouped_of, x_mx_of = {}, {}, {}
-        g_raw_of, g_grouped_of, g_mx_of = {}, {}, {}
+        g_raw_of, g_grouped_of, g_mx_of, g_stage_of = {}, {}, {}, {}
 
         def in_range(c):
             return 0 <= c < PASSES
@@ -112,7 +121,9 @@ def tile_relativemultiheadattention_pa_k_kernel(tc, pos_embed, W_r, b_r, grad_ou
                 zero_j = PACK - lag_of(c)
                 nc.vector.tensor_scalar_mul(out=x_raw[:, zero_j, :], in0=x_raw[:, zero_j, :], scalar1=keep[:, 0:1])
             x_grouped = work.tile([P, D_IN, PACK], BF16, align_bytes=64)
-            to_view, from_view = regrouped_views(x_grouped, x_raw)
+            to_view, from_view = regrouped_views(x_grouped, x_raw, V_COLS, D_IN)
+            nc.scalar.copy(out=to_view, in_=from_view)
+            to_view, from_view = regrouped_views(x_grouped, x_raw, 0, V_COLS)
             nc.vector.tensor_copy(out=to_view, in_=from_view)
             x_grouped_of[c] = x_grouped
 
@@ -138,11 +149,38 @@ def tile_relativemultiheadattention_pa_k_kernel(tc, pos_embed, W_r, b_r, grad_ou
             )
             g_raw_of[c] = g_raw
 
+        def stage_g(c):
+            if not in_range(c):
+                return
+            g_raw = g_raw_of[c]
+            g_stage = stage_pool.tile([P, STAGE_COLS, PACK], BF16)
+            if FORM == 1 or (FORM == 0 and c % 2 == 0):
+                for j in range(0, PACK, 2):
+                    nc.tensor.matmul(
+                        out=g_stage[:, 0:PE_COLS, j : j + 2],
+                        lhsT=identity[:],
+                        rhs=g_raw[:, j : j + 2, 0:PE_COLS].rearrange("p j c -> p c j"),
+                        start=True,
+                        stop=True,
+                    )
+            else:
+                for lo in range(0, PE_COLS, P):
+                    hi = min(lo + P, PE_COLS)
+                    nc.tensor.matmul(
+                        out=g_stage[:, lo:hi, :],
+                        lhsT=identity[:],
+                        rhs=g_raw[:, :, lo:hi].rearrange("p j c -> p c j"),
+                        start=True,
+                        stop=True,
+                    )
+            g_stage_of[c] = g_stage
+
         def regroup_g(c):
             if not in_range(c):
                 return
             g_grouped = work.tile([P, D_OUT, PACK], BF16, align_bytes=64)
-            to_view, from_view = regrouped_views(g_grouped, g_raw_of[c])
+            nc.scalar.copy(out=g_grouped[:, 0:PE_COLS, :], in_=g_stage_of[c][:, 0:PE_COLS, :])
+            to_view, from_view = regrouped_views(g_grouped, g_raw_of[c], PE_COLS, D_OUT)
             nc.scalar.copy(out=to_view, in_=from_view)
             g_grouped_of[c] = g_grouped
 
@@ -175,13 +213,14 @@ def tile_relativemultiheadattention_pa_k_kernel(tc, pos_embed, W_r, b_r, grad_ou
                     stop=(c == PASSES - 1),
                 )
 
-        for c in range(-1, PASSES):
-            if not is_seam(c + 1):
-                load_x(c + 1)
-            load_g(c + 1)
-            if is_seam(c + 1 + SEAM_LEAD):
-                load_x(c + 1 + SEAM_LEAD)
-            patch_x(c + 1 + SEAM_LEAD - PATCH_LAG)
+        for c in range(-LOAD_LEAD, PASSES):
+            if not is_seam(c + LOAD_LEAD):
+                load_x(c + LOAD_LEAD)
+            load_g(c + LOAD_LEAD)
+            if is_seam(c + LOAD_LEAD + SEAM_LEAD):
+                load_x(c + LOAD_LEAD + SEAM_LEAD)
+            patch_x(c + LOAD_LEAD + SEAM_LEAD - PATCH_LAG)
+            stage_g(c + STAGE_LEAD)
             regroup_g(c)
             regroup_x(c + 1)
             quantise_x(c)

@@ -21,7 +21,7 @@ M_TILES = D_OUT // P
 RUN = 4
 
 PE_COLS = 192
-V_COLS = 432
+V_COLS = 448
 STAGE_COLS = 256
 FORM = 2
 
@@ -179,9 +179,9 @@ def tile_relativemultiheadattention_pa_k_kernel(tc, pos_embed, W_r, b_r, grad_ou
             if not in_range(c):
                 return
             g_grouped = work.tile([P, D_OUT, PACK], BF16, align_bytes=64)
-            nc.scalar.copy(out=g_grouped[:, 0:PE_COLS, :], in_=g_stage_of[c][:, 0:PE_COLS, :])
             to_view, from_view = regrouped_views(g_grouped, g_raw_of[c], PE_COLS, D_OUT)
             nc.scalar.copy(out=to_view, in_=from_view)
+            nc.scalar.copy(out=g_grouped[:, 0:PE_COLS, :], in_=g_stage_of[c][:, 0:PE_COLS, :])
             g_grouped_of[c] = g_grouped
 
         def quantise_g(c):

@@ -21,7 +21,7 @@ M_TILES = D_OUT // P
 RUN = 4
 
 PE_COLS = 192
-V_COLS = 448
+V_COLS = 464
 STAGE_COLS = 256
 FORM = 2
 
@@ -181,7 +181,10 @@ def tile_relativemultiheadattention_pa_k_kernel(tc, pos_embed, W_r, b_r, grad_ou
             g_grouped = work.tile([P, D_OUT, PACK], BF16, align_bytes=64)
             to_view, from_view = regrouped_views(g_grouped, g_raw_of[c], PE_COLS, D_OUT)
             nc.scalar.copy(out=to_view, in_=from_view)
-            nc.scalar.copy(out=g_grouped[:, 0:PE_COLS, :], in_=g_stage_of[c][:, 0:PE_COLS, :])
+            nc.scalar.copy(
+                out=g_grouped[:].rearrange("p w j -> p (w j)")[:, 0 : PE_COLS * PACK].bitcast(F32),
+                in_=g_stage_of[c][:].rearrange("p w j -> p (w j)")[:, 0 : PE_COLS * PACK].bitcast(F32),
+            )
             g_grouped_of[c] = g_grouped
 
         def quantise_g(c):

@@ -21,12 +21,12 @@ M_TILES = D_OUT // P
 RUN = 4
 
 PE_COLS = 192
-V_COLS = 464
+V_COLS = 448
 STAGE_COLS = 256
 FORM = 2
 
 LOAD_LEAD = 3
-STAGE_LEAD = 2
+STAGE_LEAD = 1
 SEAM_LEAD = 4
 PATCH_LAG = 2
 
@@ -192,11 +192,13 @@ def tile_relativemultiheadattention_pa_k_kernel(tc, pos_embed, W_r, b_r, grad_ou
                 return
             g_words = work.tile([P, D_OUT], U32, align_bytes=64)
             g_scales = work.tile([P, D_OUT], U8, align_bytes=64)
-            nc.vector.quantize_mx(
-                out=g_words[:].bitcast(E5M2_X4),
-                scales=g_scales[:],
-                in_=g_grouped_of[c][:].rearrange("p w j -> p (w j)"),
-            )
+            width = P if c == PASSES - 1 else D_OUT
+            for lo in range(0, D_OUT, width):
+                nc.vector.quantize_mx(
+                    out=g_words[:, lo : lo + width].bitcast(E5M2_X4),
+                    scales=g_scales[:, lo : lo + width],
+                    in_=g_grouped_of[c][:].rearrange("p w j -> p (w j)")[:, lo * PACK : (lo + width) * PACK],
+                )
             g_mx_of[c] = (g_words, g_scales)
 
         def multiply(c):
@@ -232,7 +234,7 @@ def tile_relativemultiheadattention_pa_k_kernel(tc, pos_embed, W_r, b_r, grad_ou
 
         for m in range(M_TILES):
             result = results.tile([P, D_IN], F32)
-            if m % 2 == 0:
+            if m % 2 == 1:
                 nc.vector.tensor_copy(out=result[:], in_=acc[m][:])
             else:
                 nc.scalar.copy(out=result[:], in_=acc[m][:])

@@ -27,8 +27,7 @@ FORM = 2
 
 LOAD_LEAD = 3
 STAGE_LEAD = 1
-SEAM_LEAD = 4
-PATCH_LAG = 2
+MEND_AT = 2
 
 RAW_BUFS = 6
 WORK_BUFS = 4
@@ -63,7 +62,6 @@ def tile_relativemultiheadattention_pa_k_kernel(tc, pos_embed, W_r, b_r, grad_ou
     with ExitStack() as stack:
         const = stack.enter_context(tc.tile_pool(name="const", bufs=1))
         raw_pool = stack.enter_context(tc.tile_pool(name="raw_pool", bufs=RAW_BUFS))
-        seam_pool = stack.enter_context(tc.tile_pool(name="seam_pool", bufs=1))
         work = stack.enter_context(tc.tile_pool(name="work", bufs=WORK_BUFS))
         results = stack.enter_context(tc.tile_pool(name="results", bufs=M_TILES))
         psum = stack.enter_context(tc.psum_pool(name="psum", bufs=1))
@@ -82,6 +80,13 @@ def tile_relativemultiheadattention_pa_k_kernel(tc, pos_embed, W_r, b_r, grad_ou
             op1=mybir.AluOpType.add,
         )
 
+        mend_of = {}
+        for c in range(PASSES):
+            if is_seam(c) and lag_of(c) > 1:
+                mend = const.tile([P, lag_of(c) - 1, D_IN], BF16, name="mend%d" % c)
+                nc.gpsimd.memset(mend[:], 0.0)
+                mend_of[c] = mend
+
         acc = []
         for m in range(M_TILES):
             acc.append(psum.tile([P, D_IN], F32, name="acc%d" % m))
@@ -95,23 +100,22 @@ def tile_relativemultiheadattention_pa_k_kernel(tc, pos_embed, W_r, b_r, grad_ou
         def load_x(c):
             if not in_range(c):
                 return
-            pool = seam_pool if is_seam(c) else raw_pool
-            x_raw = pool.tile([P, PACK, D_IN], BF16)
+            x_raw = raw_pool.tile([P, PACK, D_IN], BF16)
             first = c * K_PASS + lag_of(c)
             nc.sync.dma_start(
                 out=x_raw[:], in_=e_rows[first : first + K_PASS, :].rearrange("(p j) w -> p j w", j=PACK)
             )
             x_raw_of[c] = x_raw
 
-        def patch_x(c):
-            if not in_range(c) or not is_seam(c) or lag_of(c) == 1:
-                return
-            behind = lag_of(c) - 1
-            next_batch = (c + 1) * K_PASS
-            nc.sync.dma_start(
-                out=x_raw_of[c][P - 1 : P, PACK - behind : PACK, :],
-                in_=e_rows[next_batch : next_batch + behind, :].rearrange("(o j) w -> o j w", o=1),
-            )
+        def load_mends():
+            for c in range(PASSES):
+                if is_seam(c) and lag_of(c) > 1:
+                    behind = lag_of(c) - 1
+                    next_batch = (c + 1) * K_PASS
+                    nc.sync.dma_start(
+                        out=mend_of[c][P - 1 : P, :, :],
+                        in_=e_rows[next_batch : next_batch + behind, :].rearrange("(o j) w -> o j w", o=1),
+                    )
 
         def regroup_x(c):
             if not in_range(c):
@@ -120,6 +124,15 @@ def tile_relativemultiheadattention_pa_k_kernel(tc, pos_embed, W_r, b_r, grad_ou
             if is_seam(c):
                 zero_j = PACK - lag_of(c)
                 nc.vector.tensor_scalar_mul(out=x_raw[:, zero_j, :], in0=x_raw[:, zero_j, :], scalar1=keep[:, 0:1])
+                if lag_of(c) > 1:
+                    nc.vector.scalar_tensor_tensor(
+                        out=x_raw[:, zero_j + 1 : PACK, :],
+                        in0=x_raw[:, zero_j + 1 : PACK, :],
+                        scalar=keep[:, 0:1],
+                        in1=mend_of[c][:],
+                        op0=mybir.AluOpType.mult,
+                        op1=mybir.AluOpType.add,
+                    )
             x_grouped = work.tile([P, D_IN, PACK], BF16, align_bytes=64)
             to_view, from_view = regrouped_views(x_grouped, x_raw, V_COLS, D_IN)
             nc.scalar.copy(out=to_view, in_=from_view)
@@ -219,12 +232,10 @@ def tile_relativemultiheadattention_pa_k_kernel(tc, pos_embed, W_r, b_r, grad_ou
                 )
 
         for c in range(-LOAD_LEAD, PASSES):
-            if not is_seam(c + LOAD_LEAD):
-                load_x(c + LOAD_LEAD)
+            load_x(c + LOAD_LEAD)
             load_g(c + LOAD_LEAD)
-            if is_seam(c + LOAD_LEAD + SEAM_LEAD):
-                load_x(c + LOAD_LEAD + SEAM_LEAD)
-            patch_x(c + LOAD_LEAD + SEAM_LEAD - PATCH_LAG)
+            if c + LOAD_LEAD == MEND_AT:
+                load_mends()
             stage_g(c + STAGE_LEAD)
             regroup_g(c)
             regroup_x(c + 1)

from contextlib import ExitStack

import concourse.mybir as mybir
from concourse.masks import make_identity

BF16 = mybir.dt.bfloat16
F32 = mybir.dt.float32
U32 = mybir.dt.uint32
U8 = mybir.dt.uint8
E4M3_X4 = mybir.dt.float8_e4m3fn_x4
E5M2_X4 = mybir.dt.float8_e5m2_x4

B, S, D_IN, D_OUT = 4, 4096, 512, 512
T = B * S
P = 128
PACK = 4
K_PASS = P * PACK
PASSES = T // K_PASS
PASSES_PER_BATCH = S // K_PASS
M_TILES = D_OUT // P
RUN = 4

PE_COLS = 192
V_COLS = 448
STAGE_COLS = 256
FORM = 2

LOAD_LEAD = 3
STAGE_LEAD = 1
MEND_AT = 2

RAW_BUFS = 6
WORK_BUFS = 4
STAGE_BUFS = 4

FLOPS = 2 * T * D_OUT * D_IN
BYTES = 2 * T * D_OUT + 2 * (T - (B - 1)) * D_IN + 4 * D_OUT * D_IN

assert B - 1 < PACK


def lag_of(c):
    return B - 1 - c // PASSES_PER_BATCH


def is_seam(c):
    return (c + 1) % PASSES_PER_BATCH == 0 and lag_of(c) > 0


def regrouped_views(grouped, raw, lo, hi):
    return (
        grouped[:, lo:hi, :].rearrange("p (c i) j -> p c j i", i=RUN),
        raw[:, :, lo:hi].rearrange("p j (c i) -> p c j i", i=RUN),
    )


def tile_relativemultiheadattention_pa_k_kernel(tc, pos_embed, W_r, b_r, grad_out, out):
    nc = tc.nc
    g_rows = grad_out.flatten_outer_dims()
    e_rows = pos_embed.flatten_outer_dims()

    with ExitStack() as stack:
        const = stack.enter_context(tc.tile_pool(name="const", bufs=1))
        raw_pool = stack.enter_context(tc.tile_pool(name="raw_pool", bufs=RAW_BUFS))
        work = stack.enter_context(tc.tile_pool(name="work", bufs=WORK_BUFS))
        results = stack.enter_context(tc.tile_pool(name="results", bufs=M_TILES))
        psum = stack.enter_context(tc.psum_pool(name="psum", bufs=1))
        stage_pool = stack.enter_context(tc.psum_pool(name="stage_pool", bufs=STAGE_BUFS))
        stack.enter_context(tc.manual_schedule())

        identity = const.tile([P, P], BF16)
        make_identity(nc, identity[:])
        keep = const.tile([P, 1], F32)
        nc.vector.tensor_scalar(
            out=keep[:],
            in0=identity[:, P - 1 : P],
            scalar1=-1.0,
            scalar2=1.0,
            op0=mybir.AluOpType.mult,
            op1=mybir.AluOpType.add,
        )

        mend_of = {}
        for c in range(PASSES):
            if is_seam(c) and lag_of(c) > 1:
                mend = const.tile([P, lag_of(c) - 1, D_IN], BF16, name="mend%d" % c)
                nc.gpsimd.memset(mend[:], 0.0)
                mend_of[c] = mend

        acc = []
        for m in range(M_TILES):
            acc.append(psum.tile([P, D_IN], F32, name="acc%d" % m))

        x_raw_of, x_grouped_of, x_mx_of = {}, {}, {}
        g_raw_of, g_grouped_of, g_mx_of, g_stage_of = {}, {}, {}, {}

        def in_range(c):
            return 0 <= c < PASSES

        def load_x(c):
            if not in_range(c):
                return
            x_raw = raw_pool.tile([P, PACK, D_IN], BF16)
            first = c * K_PASS + lag_of(c)
            nc.sync.dma_start(
                out=x_raw[:], in_=e_rows[first : first + K_PASS, :].rearrange("(p j) w -> p j w", j=PACK)
            )
            x_raw_of[c] = x_raw

        def load_mends():
            for c in range(PASSES):
                if is_seam(c) and lag_of(c) > 1:
                    behind = lag_of(c) - 1
                    next_batch = (c + 1) * K_PASS
                    nc.sync.dma_start(
                        out=mend_of[c][P - 1 : P, :, :],
                        in_=e_rows[next_batch : next_batch + behind, :].rearrange("(o j) w -> o j w", o=1),
                    )

        def regroup_x(c):
            if not in_range(c):
                return
            x_raw = x_raw_of[c]
            if is_seam(c):
                zero_j = PACK - lag_of(c)
                nc.vector.tensor_scalar_mul(out=x_raw[:, zero_j, :], in0=x_raw[:, zero_j, :], scalar1=keep[:, 0:1])
                if lag_of(c) > 1:
                    nc.vector.scalar_tensor_tensor(
                        out=x_raw[:, zero_j + 1 : PACK, :],
                        in0=x_raw[:, zero_j + 1 : PACK, :],
                        scalar=keep[:, 0:1],
                        in1=mend_of[c][:],
                        op0=mybir.AluOpType.mult,
                        op1=mybir.AluOpType.add,
                    )
            x_grouped = work.tile([P, D_IN, PACK], BF16, align_bytes=64)
            to_view, from_view = regrouped_views(x_grouped, x_raw, V_COLS, D_IN)
            nc.scalar.copy(out=to_view, in_=from_view)
            to_view, from_view = regrouped_views(x_grouped, x_raw, 0, V_COLS)
            nc.vector.tensor_copy(out=to_view, in_=from_view)
            x_grouped_of[c] = x_grouped

        def quantise_x(c):
            if not in_range(c):
                return
            x_words = work.tile([P, D_IN], U32, align_bytes=64)
            x_scales = work.tile([P, D_IN], U8, align_bytes=64)
            nc.vector.quantize_mx(
                out=x_words[:].bitcast(E4M3_X4),
                scales=x_scales[:],
                in_=x_grouped_of[c][:].rearrange("p w j -> p (w j)"),
            )
            x_mx_of[c] = (x_words, x_scales)

        def load_g(c):
            if not in_range(c):
                return
            g_raw = raw_pool.tile([P, PACK, D_OUT], BF16)
            first = c * K_PASS
            nc.sync.dma_start(
                out=g_raw[:], in_=g_rows[first : first + K_PASS, :].rearrange("(p j) w -> p j w", j=PACK)
            )
            g_raw_of[c] = g_raw

        def stage_g(c):
            if not in_range(c):
                return
            g_raw = g_raw_of[c]
            g_stage = stage_pool.tile([P, STAGE_COLS, PACK], BF16)
            if FORM == 1 or (FORM == 0 and c % 2 == 0):
                for j in range(0, PACK, 2):
                    nc.tensor.matmul(
                        out=g_stage[:, 0:PE_COLS, j : j + 2],
                        lhsT=identity[:],
                        rhs=g_raw[:, j : j + 2, 0:PE_COLS].rearrange("p j c -> p c j"),
                        start=True,
                        stop=True,
                    )
            else:
                for lo in range(0, PE_COLS, P):
                    hi = min(lo + P, PE_COLS)
                    nc.tensor.matmul(
                        out=g_stage[:, lo:hi, :],
                        lhsT=identity[:],
                        rhs=g_raw[:, :, lo:hi].rearrange("p j c -> p c j"),
                        start=True,
                        stop=True,
                    )
            g_stage_of[c] = g_stage

        def regroup_g(c):
            if not in_range(c):
                return
            g_grouped = work.tile([P, D_OUT, PACK], BF16, align_bytes=64)
            to_view, from_view = regrouped_views(g_grouped, g_raw_of[c], PE_COLS, D_OUT)
            nc.scalar.copy(out=to_view, in_=from_view)
            nc.scalar.copy(
                out=g_grouped[:].rearrange("p w j -> p (w j)")[:, 0 : PE_COLS * PACK].bitcast(F32),
                in_=g_stage_of[c][:].rearrange("p w j -> p (w j)")[:, 0 : PE_COLS * PACK].bitcast(F32),
            )
            g_grouped_of[c] = g_grouped

        def quantise_g(c):
            if not in_range(c):
                return
            g_words = work.tile([P, D_OUT], U32, align_bytes=64)
            g_scales = work.tile([P, D_OUT], U8, align_bytes=64)
            width = P if c == PASSES - 1 else D_OUT
            for lo in range(0, D_OUT, width):
                nc.vector.quantize_mx(
                    out=g_words[:, lo : lo + width].bitcast(E5M2_X4),
                    scales=g_scales[:, lo : lo + width],
                    in_=g_grouped_of[c][:].rearrange("p w j -> p (w j)")[:, lo * PACK : (lo + width) * PACK],
                )
            g_mx_of[c] = (g_words, g_scales)

        def multiply(c):
            if not in_range(c):
                return
            g_words, g_scales = g_mx_of[c]
            x_words, x_scales = x_mx_of[c]
            for m in range(M_TILES):
                m_cols = slice(m * P, (m + 1) * P)
                nc.tensor.matmul_mx(
                    out=acc[m][:],
                    lhsT=g_words[:, m_cols].bitcast(E5M2_X4),
                    lhsT_scale=g_scales[:, m_cols],
                    rhs=x_words[:].bitcast(E4M3_X4),
                    rhs_scale=x_scales[:],
                    start=(c == 0),
                    stop=(c == PASSES - 1),
                )

        for c in range(-LOAD_LEAD, PASSES):
            load_x(c + LOAD_LEAD)
            load_g(c + LOAD_LEAD)
            if c + LOAD_LEAD == MEND_AT:
                load_mends()
            stage_g(c + STAGE_LEAD)
            regroup_g(c)
            regroup_x(c + 1)
            quantise_x(c)
            quantise_g(c)
            multiply(c)

        for m in range(M_TILES):
            result = results.tile([P, D_IN], F32)
            if m % 2 == 1:
                nc.vector.tensor_copy(out=result[:], in_=acc[m][:])
            else:
                nc.scalar.copy(out=result[:], in_=acc[m][:])
            nc.sync.dma_start(out=out[m * P : (m + 1) * P, :], in_=result[:])
